import numpy as np
import ml_dtypes


def mxq(x, axis, fmt="e4m3"):
    dtype, down = {"e4m3": (ml_dtypes.float8_e4m3fn, 7), "e5m2": (ml_dtypes.float8_e5m2, 14)}[fmt]
    v = np.moveaxis(np.asarray(x, np.float32).astype(ml_dtypes.bfloat16).astype(np.float64), axis, -1)
    blocks = v.reshape(v.shape[:-1] + (-1, 32))
    amax = np.abs(blocks).max(-1, keepdims=True)
    byte = np.maximum(np.where(amax > 0, np.frexp(amax)[1] - 1 + 127, 0) - down, 1)
    scale = np.exp2(byte - 127.0)
    codes = (blocks / scale).astype(np.float32).astype(dtype).astype(np.float64)
    return np.moveaxis((codes * scale).reshape(v.shape), -1, axis)


WIDE = False


def mx_kscale(k):
    if not WIDE:
        return np.ones(k)
    levels = np.array([10, -10, 5, -5, 0])
    if k % 512:
        return np.exp2(np.random.permutation(np.resize(levels, k // 32))).repeat(32)
    a = np.empty((k // 512, 16))
    for p in range(k // 512):
        a[p, :8] = np.random.permutation(np.resize(levels, 8))
        for g in range(8):
            far = levels[np.abs(levels - a[p, g]) >= 10]
            a[p, g + 8] = far[np.random.randint(len(far))]
    return np.exp2(a.ravel()).repeat(32)


BF16 = ml_dtypes.bfloat16


def bf(x):
    return np.asarray(x, np.float32).astype(BF16)


def f64(x):
    return np.asarray(x).astype(np.float64)


B, M, H_ENC, N, H_DEC = 8192, 512, 512, 128, 128
SNR = 25.0
NOISE_STD = float(np.sqrt(1.0 / (2.0 * 10.0 ** (SNR / 10.0))))


def setup_inputs():
    s = mx_kscale(M)
    t = mx_kscale(H_ENC)
    theta = np.random.uniform(0.3, 1.2)
    return {"x": bf(np.random.standard_normal((B, M)) * s),
            "noise": bf(np.random.standard_normal((B, N)) * NOISE_STD),
            "h": bf(np.array([np.cos(theta), np.sin(theta)])),
            "W1": bf(np.random.standard_normal((H_ENC, M)) / np.sqrt(M) / s[None, :] * t[:, None]),
            "b1": bf(np.random.standard_normal(H_ENC) * 0.3 * t),
            "W2": bf(np.random.standard_normal((N, H_ENC)) / np.sqrt(H_ENC) / t[None, :]),
            "b2": bf(np.random.standard_normal(N) * 0.3)}


def reference(x, noise, h, W1, b1, W2, b2):
    h = f64(h)
    a = np.maximum((mxq(f64(x), 1, "e4m3") @ mxq(f64(W1), 1, "e4m3").T) + f64(b1), 0.0)
    z = (mxq(a, 1, "e4m3") @ mxq(f64(W2), 1, "e4m3").T) + f64(b2)
    scale = np.sqrt(N * 0.5)
    z = scale * z / np.linalg.norm(z, axis=1, keepdims=True)
    zc = z.reshape(B, N // 2, 2)
    yr = zc[..., 0] * h[0] - zc[..., 1] * h[1]
    yi = zc[..., 0] * h[1] + zc[..., 1] * h[0]
    y = np.stack([yr, yi], axis=-1).reshape(B, N)
    return y + f64(noise)

@@ -1,0 +1,287 @@
+from contextlib import ExitStack
+
+import concourse.masks as masks
+import concourse.mybir as mybir
+
+F32 = mybir.dt.float32
+BF16 = mybir.dt.bfloat16
+U32 = mybir.dt.uint32
+U8 = mybir.dt.uint8
+FP8X4 = mybir.dt.float8_e4m3fn_x4
+ACT = mybir.ActivationFunctionType
+ALU = mybir.AluOpType
+
+P = 128
+PACK = 4
+BATCH, D_IN, D_HID, D_OUT = 8192, 512, 512, 128
+CHUNK = 512
+TILES = CHUNK // P
+NCHUNK = BATCH // CHUNK
+ROWS_PER_PARTITION = BATCH // P
+NOISE_TILES = 16
+TINY = 1e-30
+
+FLOPS = 2 * BATCH * D_IN * D_HID + 2 * BATCH * D_HID * D_OUT
+
+
+def tile_channel_net_pa_kernel(tc, x, noise, h, W1, b1, W2, b2, out):
+    nc = tc.nc
+    with ExitStack() as ctx:
+        ctx.enter_context(tc.manual_schedule())
+        keep = ctx.enter_context(tc.tile_pool(name="keep", bufs=1))
+        work = ctx.enter_context(tc.tile_pool(name="work", bufs=3))
+        psum_t = ctx.enter_context(tc.psum_pool(name="psum_t", bufs=2))
+        psum_a = ctx.enter_context(tc.psum_pool(name="psum_a", bufs=PACK))
+        psum_e = ctx.enter_context(tc.psum_pool(name="psum_e", bufs=1))
+
+        h_bf = keep.tile([P, 2], BF16)
+        b1_bf = keep.tile([P, PACK], BF16)
+        b2_bf = keep.tile([P, 1], BF16)
+        with nc.allow_non_contiguous_dma(reason="three vectors of at most 1 KiB"):
+            nc.scalar.dma_start(out=b1_bf[:], in_=b1.rearrange("(q t) -> q t", t=PACK))
+            nc.scalar.dma_start(out=h_bf[:], in_=h.partition_broadcast(P))
+            nc.scalar.dma_start(out=b2_bf[:], in_=b2.rearrange("(q o) -> q o", o=1))
+
+        w2_sb = keep.tile([P, D_HID], BF16)
+        nc.sync.dma_start(out=w2_sb[:], in_=W2)
+        w1_sb = keep.tile([P, PACK * D_IN], BF16)
+        nc.sync.dma_start(out=w1_sb[:], in_=W1.rearrange("(q t) k -> q (t k)", t=PACK))
+        x_cols = x.rearrange("(p r) k -> p (r k)", r=ROWS_PER_PARTITION)
+        noise_rows = noise.rearrange("(p r) n -> p r n", r=ROWS_PER_PARTITION)
+        out_rows = out.rearrange("(p r) n -> p r n", r=ROWS_PER_PARTITION)
+        x_sb = []
+        noise_sb = []
+        for c in range(NCHUNK):
+            x_c = keep.tile([P, TILES * D_IN], BF16, name="x%d" % c)
+            nc.sync.dma_start(out=x_c[:], in_=x_cols[:, c * TILES * D_IN : (c + 1) * TILES * D_IN])
+            x_sb.append(x_c)
+            if (c * TILES) % NOISE_TILES == 0:
+                first = c * TILES
+                n_c = keep.tile([P, NOISE_TILES, D_OUT], BF16, name="noise%d" % c)
+                nc.sync.dma_start(out=n_c[:], in_=noise_rows[:, first : first + NOISE_TILES, :])
+                noise_sb.append(n_c)
+
+        ident = keep.tile([P, P], F32)
+        masks.make_identity(nc, ident[:])
+
+        one = keep.tile([P, 1], F32)
+        nc.vector.memset(one[:], 1.0)
+        one_root = keep.tile([P, 1], F32)
+        nc.scalar.activation(out=one_root[:], in_=one[:], func=ACT.Abs_reciprocal_sqrt)
+
+        b1_f = keep.tile([P, PACK], F32)
+        nc.vector.tensor_copy(out=b1_f[:], in_=b1_bf[:])
+        b2_f = keep.tile([P, 1], F32)
+        nc.vector.tensor_copy(out=b2_f[:], in_=b2_bf[:])
+        h_f = keep.tile([P, 2], F32)
+        nc.vector.tensor_copy(out=h_f[:], in_=h_bf[:])
+        h_re = h_f[:, 0:1]
+        h_im = h_f[:, 1:2]
+        h_im_neg = keep.tile([P, 1], F32)
+        nc.vector.tensor_scalar(
+            out=h_im_neg[:], in0=h_im, scalar1=-1.0, scalar2=None, op0=ALU.mult
+        )
+
+        h_sq = keep.tile([P, 2], F32)
+        nc.vector.tensor_tensor(out=h_sq[:], in0=h_f[:], in1=h_f[:], op=ALU.mult)
+        h_abs2 = keep.tile([P, 1], F32)
+        nc.vector.tensor_tensor(out=h_abs2[:], in0=h_sq[:, 0:1], in1=h_sq[:, 1:2], op=ALU.add)
+        gain2 = keep.tile([P, 1], F32)
+        nc.vector.tensor_scalar(
+            out=gain2[:], in0=h_abs2[:], scalar1=float(D_OUT // 2), scalar2=TINY,
+            op0=ALU.mult, op1=ALU.max,
+        )
+        inv_gain2 = keep.tile([P, 1], F32)
+        nc.vector.reciprocal(out=inv_gain2[:], in_=gain2[:])
+
+        tap_diag = keep.tile([P, P], F32)
+        nc.vector.tensor_scalar(
+            out=tap_diag[:], in0=ident[:], scalar1=h_re, scalar2=None, op0=ALU.mult
+        )
+        tap = keep.tile([P, P], F32)
+        ident_pairs = ident[:].rearrange("n (j e) -> n j e", e=2)
+        diag_pairs = tap_diag[:].rearrange("n (j e) -> n j e", e=2)
+        tap_pairs = tap[:].rearrange("n (j e) -> n j e", e=2)
+        nc.vector.scalar_tensor_tensor(
+            out=tap_pairs[:, :, 0], in0=ident_pairs[:, :, 1], scalar=h_im_neg[:],
+            in1=diag_pairs[:, :, 0], op0=ALU.mult, op1=ALU.add,
+        )
+        nc.vector.scalar_tensor_tensor(
+            out=tap_pairs[:, :, 1], in0=ident_pairs[:, :, 0], scalar=h_im,
+            in1=diag_pairs[:, :, 1], op0=ALU.mult, op1=ALU.add,
+        )
+
+        def transpose_block(rows):
+            words = rows[:].bitcast(F32).rearrange("b (i q u) -> b i u q", i=TILES, u=2)
+            banks = []
+            for pair in range(TILES // 2):
+                bank = psum_t.tile([P, 2, 2, P], F32, name="xt", tag="xt")
+                for i in range(2):
+                    for u in range(2):
+                        nc.tensor.transpose(
+                            bank[:, i, u, :], words[:, 2 * pair + i, u, :], ident[:]
+                        )
+                banks.append(bank)
+            return banks
+
+        def interleave_block(banks, grouped, copies):
+            words = grouped[:].bitcast(F32).rearrange("q (i b u) -> q i b u", i=TILES, u=2)
+            for pair in range(TILES // 2):
+                copies[pair](
+                    out=words[:, 2 * pair : 2 * pair + 2, :, :],
+                    in_=banks[pair][:].rearrange("q i u b -> q i b u"),
+                )
+
+        def quantise(grouped, codes, scales):
+            nc.vector.quantize_mx(out=codes[:].bitcast(FP8X4), scales=scales[:], in_=grouped[:])
+
+        w2_words = w2_sb[:].bitcast(F32).rearrange("n (q u) -> n u q", u=2)
+        w2_bank = psum_t.tile([P, 2, 2, P], F32, name="xt", tag="xt")
+        for u in range(2):
+            nc.tensor.transpose(w2_bank[:, 0, u, :], w2_words[:, u, :], ident[:])
+        w2_grouped = keep.tile([P, D_OUT * PACK], BF16, align_bytes=64)
+        nc.scalar.copy(
+            out=w2_grouped[:].bitcast(F32).rearrange("q (n u) -> q n u", u=2),
+            in_=w2_bank[:, 0, :, :].rearrange("q u n -> q n u"),
+        )
+        w2_codes = keep.tile([P, D_OUT], U32, align_bytes=64)
+        w2_scales = keep.tile([P, D_OUT], U8, align_bytes=64)
+        quantise(w2_grouped, w2_codes, w2_scales)
+
+        x_banks, x_grouped, x_codes, x_scales = {}, {}, {}, {}
+        a_banks, a_planes, a_grouped, a_codes, a_scales = {}, {}, {}, {}, {}
+        zt_bank, zt_sb, y_bank, y_sums, y_scale = {}, {}, {}, {}, {}
+
+        def transpose_x(c):
+            x_banks[c] = transpose_block(x_sb[c])
+
+        def interleave_x(c):
+            x_grouped[c] = work.tile([P, CHUNK * PACK], BF16, name="x_grouped", align_bytes=64)
+            second = nc.scalar.copy if c % 2 == 1 else nc.vector.tensor_copy
+            interleave_block(x_banks[c], x_grouped[c], (nc.vector.tensor_copy, second))
+
+        def quantise_x(c):
+            x_codes[c] = work.tile([P, CHUNK], U32, name="x_codes", align_bytes=64)
+            x_scales[c] = work.tile([P, CHUNK], U8, name="x_scales", align_bytes=64)
+            quantise(x_grouped[c], x_codes[c], x_scales[c])
+
+        def layer1(c):
+            a_banks[c] = []
+            for t in range(PACK):
+                bank = psum_a.tile([P, CHUNK], F32, name="a_bank", tag="a_bank")
+                units = slice(t * P, (t + 1) * P)
+                nc.tensor.matmul_mx(
+                    out=bank[:],
+                    lhsT=w1_codes[:, units].bitcast(FP8X4),
+                    lhsT_scale=w1_scales[:, units],
+                    rhs=x_codes[c][:].bitcast(FP8X4),
+                    rhs_scale=x_scales[c][:],
+                    start=True,
+                    stop=True,
+                )
+                a_banks[c].append(bank)
+
+        def relu(c):
+            a_planes[c] = work.tile([P, PACK, CHUNK], BF16, name="a_planes")
+            for t in range(PACK):
+                nc.scalar.activation(
+                    out=a_planes[c][:, t, :], in_=a_banks[c][t][:], func=ACT.Relu,
+                    bias=b1_f[:, t : t + 1], scale=1.0,
+                )
+
+        def regroup_a(c):
+            a_grouped[c] = work.tile([P, CHUNK, PACK], BF16, name="a_grouped", align_bytes=64)
+            nc.vector.tensor_copy(
+                out=a_grouped[c][:].rearrange("q (c i) t -> q c t i", i=4),
+                in_=a_planes[c][:].rearrange("q t (c i) -> q c t i", i=4),
+            )
+
+        def quantise_a(c):
+            a_codes[c] = work.tile([P, CHUNK], U32, name="a_codes", align_bytes=64)
+            a_scales[c] = work.tile([P, CHUNK], U8, name="a_scales", align_bytes=64)
+            nc.vector.quantize_mx(
+                out=a_codes[c][:].bitcast(FP8X4),
+                scales=a_scales[c][:],
+                in_=a_grouped[c][:].rearrange("q b t -> q (b t)"),
+            )
+
+        def layer2(c):
+            zt_bank[c] = psum_e.tile([P, CHUNK], F32, name="zt_bank", tag="end%d" % (c % 2))
+            nc.tensor.matmul_mx(
+                out=zt_bank[c][:],
+                lhsT=w2_codes[:].bitcast(FP8X4),
+                lhsT_scale=w2_scales[:],
+                rhs=a_codes[c][:].bitcast(FP8X4),
+                rhs_scale=a_scales[c][:],
+                start=True,
+                stop=True,
+            )
+
+        def add_b2(c):
+            zt_sb[c] = work.tile([P, CHUNK], F32, name="zt_sb")
+            nc.scalar.activation(
+                out=zt_sb[c][:], in_=zt_bank[c][:], func=ACT.Identity, bias=b2_f[:], scale=1.0
+            )
+
+        def rotate(c):
+            y_bank[c] = psum_e.tile([P, TILES, D_OUT], F32, name="y_bank", tag="end%d" % (c % 2))
+            for i in range(TILES):
+                nc.tensor.matmul(
+                    out=y_bank[c][:, i, :], lhsT=zt_sb[c][:, i * P : (i + 1) * P], rhs=tap[:],
+                    start=True, stop=True,
+                )
+
+        def sum_squares(c):
+            squares = work.tile([P, TILES, D_OUT], BF16, name="squares")
+            y_sums[c] = work.tile([P, TILES], F32, name="y_sums")
+            for i in range(TILES):
+                nc.scalar.activation(
+                    out=squares[:, i, :], in_=y_bank[c][:, i, :], func=ACT.Square,
+                    accum_out=y_sums[c][:, i : i + 1],
+                )
+
+        def invert_norms(c):
+            y_scale[c] = work.tile([P, TILES], F32, name="y_scale")
+            nc.scalar.activation(
+                out=y_scale[c][:], in_=y_sums[c][:], func=ACT.Abs_reciprocal_sqrt,
+                bias=TINY, scale=inv_gain2[:],
+            )
+
+        def finish(c):
+            result = work.tile([P, TILES, D_OUT], F32, name="result")
+            for i in range(TILES):
+                r = c * TILES + i
+                nc.vector.scalar_tensor_tensor(
+                    out=result[:, i, :], in0=y_bank[c][:, i, :], scalar=y_scale[c][:, i : i + 1],
+                    in1=noise_sb[r // NOISE_TILES][:, r % NOISE_TILES, :],
+                    op0=ALU.mult, op1=ALU.add,
+                )
+            nc.sync.dma_start(out=out_rows[:, c * TILES : (c + 1) * TILES, :], in_=result[:])
+
+        def run(stage, c):
+            if 0 <= c < NCHUNK:
+                stage(c)
+
+        w1_banks = transpose_block(w1_sb)
+        w1_grouped = keep.tile([P, CHUNK * PACK], BF16, align_bytes=64)
+        interleave_block(w1_banks, w1_grouped, (nc.scalar.copy, nc.scalar.copy))
+        transpose_x(0)
+        interleave_x(0)
+        w1_codes = keep.tile([P, D_HID], U32, align_bytes=64)
+        w1_scales = keep.tile([P, D_HID], U8, align_bytes=64)
+        quantise(w1_grouped, w1_codes, w1_scales)
+
+        for step in range(-1, NCHUNK + 3):
+            run(transpose_x, step + 2)
+            run(finish, step - 3)
+            run(rotate, step - 2)
+            run(quantise_a, step - 1)
+            run(layer2, step - 1)
+            run(quantise_x, step + 1)
+            run(relu, step)
+            run(layer1, step + 1)
+            run(interleave_x, step + 2)
+            run(sum_squares, step - 2)
+            run(add_b2, step - 1)
+            run(invert_norms, step - 2)
+            run(regroup_a, step)

@@ -16,8 +16,10 @@ PACK = 4
 BATCH, D_IN, D_HID, D_OUT = 8192, 512, 512, 128
 CHUNK = 512
 TILES = CHUNK // P
-NCHUNK = BATCH // CHUNK
 ROWS_PER_PARTITION = BATCH // P
+SIZES = [TILES // 2] + [TILES] * (ROWS_PER_PARTITION // TILES - 1) + [TILES // 2]
+FIRSTS = [sum(SIZES[:c]) for c in range(len(SIZES))]
+NCHUNK = len(SIZES)
 NOISE_TILES = 16
 TINY = 1e-30
 
@@ -42,24 +44,34 @@ def tile_channel_net_pa_kernel(tc, x, noise, h, W1, b1, W2, b2, out):
             nc.scalar.dma_start(out=h_bf[:], in_=h.partition_broadcast(P))
             nc.scalar.dma_start(out=b2_bf[:], in_=b2.rearrange("(q o) -> q o", o=1))
 
-        w2_sb = keep.tile([P, D_HID], BF16)
-        nc.sync.dma_start(out=w2_sb[:], in_=W2)
-        w1_sb = keep.tile([P, PACK * D_IN], BF16)
-        nc.sync.dma_start(out=w1_sb[:], in_=W1.rearrange("(q t) k -> q (t k)", t=PACK))
         x_cols = x.rearrange("(p r) k -> p (r k)", r=ROWS_PER_PARTITION)
         noise_rows = noise.rearrange("(p r) n -> p r n", r=ROWS_PER_PARTITION)
         out_rows = out.rearrange("(p r) n -> p r n", r=ROWS_PER_PARTITION)
+        w1_rows = W1.rearrange("(q t) k -> q t k", t=PACK)
+        w1_sb = []
+        w2_sb = keep.tile([P, D_HID], BF16)
         x_sb = []
         noise_sb = []
         for c in range(NCHUNK):
-            x_c = keep.tile([P, TILES * D_IN], BF16, name="x%d" % c)
-            nc.sync.dma_start(out=x_c[:], in_=x_cols[:, c * TILES * D_IN : (c + 1) * TILES * D_IN])
+            first = FIRSTS[c]
+            x_c = keep.tile([P, SIZES[c] * D_IN], BF16, name="x%d" % c)
+            nc.sync.dma_start(
+                out=x_c[:], in_=x_cols[:, first * D_IN : (first + SIZES[c]) * D_IN]
+            )
             x_sb.append(x_c)
-            if (c * TILES) % NOISE_TILES == 0:
-                first = c * TILES
-                n_c = keep.tile([P, NOISE_TILES, D_OUT], BF16, name="noise%d" % c)
-                nc.sync.dma_start(out=n_c[:], in_=noise_rows[:, first : first + NOISE_TILES, :])
-                noise_sb.append(n_c)
+            if c == 0:
+                for t in range(PACK):
+                    w1_t = keep.tile([P, D_IN], BF16, name="w1_%d" % t)
+                    nc.sync.dma_start(out=w1_t[:], in_=w1_rows[:, t, :])
+                    w1_sb.append(w1_t)
+                nc.sync.dma_start(out=w2_sb[:], in_=W2)
+            while len(noise_sb) * NOISE_TILES + NOISE_TILES // 2 < first + SIZES[c]:
+                n_first = len(noise_sb) * NOISE_TILES
+                n_g = keep.tile([P, NOISE_TILES, D_OUT], BF16, name="noise%d" % len(noise_sb))
+                nc.sync.dma_start(
+                    out=n_g[:], in_=noise_rows[:, n_first : n_first + NOISE_TILES, :]
+                )
+                noise_sb.append(n_g)
 
         ident = keep.tile([P, P], F32)
         masks.make_identity(nc, ident[:])
@@ -71,111 +83,114 @@ def tile_channel_net_pa_kernel(tc, x, noise, h, W1, b1, W2, b2, out):
 
         b1_f = keep.tile([P, PACK], F32)
         nc.vector.tensor_copy(out=b1_f[:], in_=b1_bf[:])
+
         b2_f = keep.tile([P, 1], F32)
-        nc.vector.tensor_copy(out=b2_f[:], in_=b2_bf[:])
+        nc.gpsimd.tensor_copy(out=b2_f[:], in_=b2_bf[:])
         h_f = keep.tile([P, 2], F32)
-        nc.vector.tensor_copy(out=h_f[:], in_=h_bf[:])
+        nc.gpsimd.tensor_copy(out=h_f[:], in_=h_bf[:])
         h_re = h_f[:, 0:1]
         h_im = h_f[:, 1:2]
         h_im_neg = keep.tile([P, 1], F32)
-        nc.vector.tensor_scalar(
+        nc.gpsimd.tensor_scalar(
             out=h_im_neg[:], in0=h_im, scalar1=-1.0, scalar2=None, op0=ALU.mult
         )
 
         h_sq = keep.tile([P, 2], F32)
-        nc.vector.tensor_tensor(out=h_sq[:], in0=h_f[:], in1=h_f[:], op=ALU.mult)
+        nc.gpsimd.tensor_tensor(out=h_sq[:], in0=h_f[:], in1=h_f[:], op=ALU.mult)
         h_abs2 = keep.tile([P, 1], F32)
-        nc.vector.tensor_tensor(out=h_abs2[:], in0=h_sq[:, 0:1], in1=h_sq[:, 1:2], op=ALU.add)
+        nc.gpsimd.tensor_tensor(out=h_abs2[:], in0=h_sq[:, 0:1], in1=h_sq[:, 1:2], op=ALU.add)
         gain2 = keep.tile([P, 1], F32)
-        nc.vector.tensor_scalar(
+        nc.gpsimd.tensor_scalar(
             out=gain2[:], in0=h_abs2[:], scalar1=float(D_OUT // 2), scalar2=TINY,
             op0=ALU.mult, op1=ALU.max,
         )
         inv_gain2 = keep.tile([P, 1], F32)
-        nc.vector.reciprocal(out=inv_gain2[:], in_=gain2[:])
 
         tap_diag = keep.tile([P, P], F32)
-        nc.vector.tensor_scalar(
-            out=tap_diag[:], in0=ident[:], scalar1=h_re, scalar2=None, op0=ALU.mult
+        nc.gpsimd.tensor_scalar(
+            out=tap_diag[:], in0=ident[:], scalar1=h_re, scalar2=0.0, op0=ALU.mult, op1=ALU.add,
         )
+        tap_cross = keep.tile([P, P], F32)
         tap = keep.tile([P, P], F32)
         ident_pairs = ident[:].rearrange("n (j e) -> n j e", e=2)
-        diag_pairs = tap_diag[:].rearrange("n (j e) -> n j e", e=2)
-        tap_pairs = tap[:].rearrange("n (j e) -> n j e", e=2)
-        nc.vector.scalar_tensor_tensor(
-            out=tap_pairs[:, :, 0], in0=ident_pairs[:, :, 1], scalar=h_im_neg[:],
-            in1=diag_pairs[:, :, 0], op0=ALU.mult, op1=ALU.add,
+        cross_pairs = tap_cross[:].rearrange("n (j e) -> n j e", e=2)
+        nc.gpsimd.tensor_scalar(
+            out=cross_pairs[:, :, 0], in0=ident_pairs[:, :, 1], scalar1=h_im_neg[:],
+            scalar2=0.0, op0=ALU.mult, op1=ALU.add,
         )
-        nc.vector.scalar_tensor_tensor(
-            out=tap_pairs[:, :, 1], in0=ident_pairs[:, :, 0], scalar=h_im,
-            in1=diag_pairs[:, :, 1], op0=ALU.mult, op1=ALU.add,
+        nc.gpsimd.tensor_scalar(
+            out=cross_pairs[:, :, 1], in0=ident_pairs[:, :, 0], scalar1=h_im,
+            scalar2=0.0, op0=ALU.mult, op1=ALU.add,
         )
+        nc.gpsimd.tensor_tensor(out=tap[:], in0=tap_diag[:], in1=tap_cross[:], op=ALU.add)
 
-        def transpose_block(rows):
-            words = rows[:].bitcast(F32).rearrange("b (i q u) -> b i u q", i=TILES, u=2)
-            banks = []
-            for pair in range(TILES // 2):
-                bank = psum_t.tile([P, 2, 2, P], F32, name="xt", tag="xt")
-                for i in range(2):
-                    for u in range(2):
-                        nc.tensor.transpose(
-                            bank[:, i, u, :], words[:, 2 * pair + i, u, :], ident[:]
-                        )
-                banks.append(bank)
-            return banks
+        def transpose_pair(rows, bank):
+            for i in range(2):
+                words = rows[i].bitcast(F32).rearrange("b (q u) -> b u q", u=2)
+                for u in range(2):
+                    nc.tensor.transpose(bank[:, i, u, :], words[:, u, :], ident[:])
 
-        def interleave_block(banks, grouped, copies):
-            words = grouped[:].bitcast(F32).rearrange("q (i b u) -> q i b u", i=TILES, u=2)
-            for pair in range(TILES // 2):
-                copies[pair](
-                    out=words[:, 2 * pair : 2 * pair + 2, :, :],
-                    in_=banks[pair][:].rearrange("q i u b -> q i b u"),
-                )
+        def interleave_pair(bank, grouped, copy):
+            copy(
+                out=grouped.bitcast(F32).rearrange("q (i b u) -> q i b u", i=2, u=2),
+                in_=bank[:].rearrange("q i u b -> q i b u"),
+            )
 
         def quantise(grouped, codes, scales):
-            nc.vector.quantize_mx(out=codes[:].bitcast(FP8X4), scales=scales[:], in_=grouped[:])
+            nc.vector.quantize_mx(out=codes.bitcast(FP8X4), scales=scales, in_=grouped)
 
-        w2_words = w2_sb[:].bitcast(F32).rearrange("n (q u) -> n u q", u=2)
-        w2_bank = psum_t.tile([P, 2, 2, P], F32, name="xt", tag="xt")
-        for u in range(2):
-            nc.tensor.transpose(w2_bank[:, 0, u, :], w2_words[:, u, :], ident[:])
+        PAIR = 2 * P
+        w1_grouped = keep.tile([P, D_HID * PACK], BF16, align_bytes=64)
+        w1_codes = keep.tile([P, D_HID], U32, align_bytes=64)
+        w1_scales = keep.tile([P, D_HID], U8, align_bytes=64)
         w2_grouped = keep.tile([P, D_OUT * PACK], BF16, align_bytes=64)
-        nc.scalar.copy(
-            out=w2_grouped[:].bitcast(F32).rearrange("q (n u) -> q n u", u=2),
-            in_=w2_bank[:, 0, :, :].rearrange("q u n -> q n u"),
-        )
         w2_codes = keep.tile([P, D_OUT], U32, align_bytes=64)
         w2_scales = keep.tile([P, D_OUT], U8, align_bytes=64)
-        quantise(w2_grouped, w2_codes, w2_scales)
 
         x_banks, x_grouped, x_codes, x_scales = {}, {}, {}, {}
         a_banks, a_planes, a_grouped, a_codes, a_scales = {}, {}, {}, {}, {}
         zt_bank, zt_sb, y_bank, y_sums, y_scale = {}, {}, {}, {}, {}
 
         def transpose_x(c):
-            x_banks[c] = transpose_block(x_sb[c])
+            x_banks[c] = []
+            for pair in range(SIZES[c] // 2):
+                bank = psum_t.tile([P, 2, 2, P], F32, name="xt", tag="xt")
+                first = 2 * pair * D_IN
+                transpose_pair(
+                    [x_sb[c][:, first : first + D_IN], x_sb[c][:, first + D_IN : first + 2 * D_IN]],
+                    bank,
+                )
+                x_banks[c].append(bank)
 
         def interleave_x(c):
             x_grouped[c] = work.tile([P, CHUNK * PACK], BF16, name="x_grouped", align_bytes=64)
-            second = nc.scalar.copy if c % 2 == 1 else nc.vector.tensor_copy
-            interleave_block(x_banks[c], x_grouped[c], (nc.vector.tensor_copy, second))
+            for pair in range(SIZES[c] // 2):
+                on_scalar = pair == 1 and c % 2 == 0
+                first = pair * PAIR * PACK
+                interleave_pair(
+                    x_banks[c][pair],
+                    x_grouped[c][:, first : first + PAIR * PACK],
+                    nc.scalar.copy if on_scalar else nc.vector.tensor_copy,
+                )
 
         def quantise_x(c):
             x_codes[c] = work.tile([P, CHUNK], U32, name="x_codes", align_bytes=64)
             x_scales[c] = work.tile([P, CHUNK], U8, name="x_scales", align_bytes=64)
-            quantise(x_grouped[c], x_codes[c], x_scales[c])
+            n = SIZES[c] * P
+            quantise(x_grouped[c][:, : n * PACK], x_codes[c][:, :n], x_scales[c][:, :n])
 
         def layer1(c):
             a_banks[c] = []
+            n = SIZES[c] * P
             for t in range(PACK):
                 bank = psum_a.tile([P, CHUNK], F32, name="a_bank", tag="a_bank")
                 units = slice(t * P, (t + 1) * P)
                 nc.tensor.matmul_mx(
-                    out=bank[:],
+                    out=bank[:, :n],
                     lhsT=w1_codes[:, units].bitcast(FP8X4),
                     lhsT_scale=w1_scales[:, units],
-                    rhs=x_codes[c][:].bitcast(FP8X4),
-                    rhs_scale=x_scales[c][:],
+                    rhs=x_codes[c][:, :n].bitcast(FP8X4),
+                    rhs_scale=x_scales[c][:, :n],
                     start=True,
                     stop=True,
                 )
@@ -183,49 +198,55 @@ def tile_channel_net_pa_kernel(tc, x, noise, h, W1, b1, W2, b2, out):
 
         def relu(c):
             a_planes[c] = work.tile([P, PACK, CHUNK], BF16, name="a_planes")
+            n = SIZES[c] * P
             for t in range(PACK):
                 nc.scalar.activation(
-                    out=a_planes[c][:, t, :], in_=a_banks[c][t][:], func=ACT.Relu,
+                    out=a_planes[c][:, t, :n], in_=a_banks[c][t][:, :n], func=ACT.Relu,
                     bias=b1_f[:, t : t + 1], scale=1.0,
                 )
 
         def regroup_a(c):
             a_grouped[c] = work.tile([P, CHUNK, PACK], BF16, name="a_grouped", align_bytes=64)
+            n = SIZES[c] * P
             nc.vector.tensor_copy(
-                out=a_grouped[c][:].rearrange("q (c i) t -> q c t i", i=4),
-                in_=a_planes[c][:].rearrange("q t (c i) -> q c t i", i=4),
+                out=a_grouped[c][:, :n, :].rearrange("q (c i) t -> q c t i", i=4),
+                in_=a_planes[c][:, :, :n].rearrange("q t (c i) -> q c t i", i=4),
             )
 
         def quantise_a(c):
             a_codes[c] = work.tile([P, CHUNK], U32, name="a_codes", align_bytes=64)
             a_scales[c] = work.tile([P, CHUNK], U8, name="a_scales", align_bytes=64)
-            nc.vector.quantize_mx(
-                out=a_codes[c][:].bitcast(FP8X4),
-                scales=a_scales[c][:],
-                in_=a_grouped[c][:].rearrange("q b t -> q (b t)"),
+            n = SIZES[c] * P
+            quantise(
+                a_grouped[c][:, :n, :].rearrange("q b t -> q (b t)"),
+                a_codes[c][:, :n],
+                a_scales[c][:, :n],
             )
 
         def layer2(c):
             zt_bank[c] = psum_e.tile([P, CHUNK], F32, name="zt_bank", tag="end%d" % (c % 2))
+            n = SIZES[c] * P
             nc.tensor.matmul_mx(
-                out=zt_bank[c][:],
+                out=zt_bank[c][:, :n],
                 lhsT=w2_codes[:].bitcast(FP8X4),
                 lhsT_scale=w2_scales[:],
-                rhs=a_codes[c][:].bitcast(FP8X4),
-                rhs_scale=a_scales[c][:],
+                rhs=a_codes[c][:, :n].bitcast(FP8X4),
+                rhs_scale=a_scales[c][:, :n],
                 start=True,
                 stop=True,
             )
 
         def add_b2(c):
             zt_sb[c] = work.tile([P, CHUNK], F32, name="zt_sb")
+            n = SIZES[c] * P
             nc.scalar.activation(
-                out=zt_sb[c][:], in_=zt_bank[c][:], func=ACT.Identity, bias=b2_f[:], scale=1.0
+                out=zt_sb[c][:, :n], in_=zt_bank[c][:, :n], func=ACT.Identity, bias=b2_f[:],
+                scale=1.0,
             )
 
         def rotate(c):
             y_bank[c] = psum_e.tile([P, TILES, D_OUT], F32, name="y_bank", tag="end%d" % (c % 2))
-            for i in range(TILES):
+            for i in range(SIZES[c]):
                 nc.tensor.matmul(
                     out=y_bank[c][:, i, :], lhsT=zt_sb[c][:, i * P : (i + 1) * P], rhs=tap[:],
                     start=True, stop=True,
@@ -234,7 +255,7 @@ def tile_channel_net_pa_kernel(tc, x, noise, h, W1, b1, W2, b2, out):
         def sum_squares(c):
             squares = work.tile([P, TILES, D_OUT], BF16, name="squares")
             y_sums[c] = work.tile([P, TILES], F32, name="y_sums")
-            for i in range(TILES):
+            for i in range(SIZES[c]):
                 nc.scalar.activation(
                     out=squares[:, i, :], in_=y_bank[c][:, i, :], func=ACT.Square,
                     accum_out=y_sums[c][:, i : i + 1],
@@ -243,35 +264,53 @@ def tile_channel_net_pa_kernel(tc, x, noise, h, W1, b1, W2, b2, out):
         def invert_norms(c):
             y_scale[c] = work.tile([P, TILES], F32, name="y_scale")
             nc.scalar.activation(
-                out=y_scale[c][:], in_=y_sums[c][:], func=ACT.Abs_reciprocal_sqrt,
-                bias=TINY, scale=inv_gain2[:],
+                out=y_scale[c][:, : SIZES[c]], in_=y_sums[c][:, : SIZES[c]],
+                func=ACT.Abs_reciprocal_sqrt, bias=TINY, scale=inv_gain2[:],
             )
 
         def finish(c):
             result = work.tile([P, TILES, D_OUT], F32, name="result")
-            for i in range(TILES):
-                r = c * TILES + i
+            for i in range(SIZES[c]):
+                r = FIRSTS[c] + i
                 nc.vector.scalar_tensor_tensor(
                     out=result[:, i, :], in0=y_bank[c][:, i, :], scalar=y_scale[c][:, i : i + 1],
                     in1=noise_sb[r // NOISE_TILES][:, r % NOISE_TILES, :],
                     op0=ALU.mult, op1=ALU.add,
                 )
-            nc.sync.dma_start(out=out_rows[:, c * TILES : (c + 1) * TILES, :], in_=result[:])
+            nc.sync.dma_start(
+                out=out_rows[:, FIRSTS[c] : FIRSTS[c] + SIZES[c], :], in_=result[:, : SIZES[c], :]
+            )
 
         def run(stage, c):
             if 0 <= c < NCHUNK:
                 stage(c)
 
-        w1_banks = transpose_block(w1_sb)
-        w1_grouped = keep.tile([P, CHUNK * PACK], BF16, align_bytes=64)
-        interleave_block(w1_banks, w1_grouped, (nc.scalar.copy, nc.scalar.copy))
         transpose_x(0)
         interleave_x(0)
-        w1_codes = keep.tile([P, D_HID], U32, align_bytes=64)
-        w1_scales = keep.tile([P, D_HID], U8, align_bytes=64)
-        quantise(w1_grouped, w1_codes, w1_scales)
+        for pair in range(PACK // 2):
+            w1_bank = psum_a.tile([P, 2, 2, P], F32, name="w1_bank", tag="a_bank")
+            transpose_pair([w1_sb[2 * pair][:], w1_sb[2 * pair + 1][:]], w1_bank)
+            words = slice(pair * PAIR, (pair + 1) * PAIR)
+            halves = slice(pair * PAIR * PACK, (pair + 1) * PAIR * PACK)
+            interleave_pair(w1_bank, w1_grouped[:, halves], nc.scalar.copy)
+            if pair == 0:
+                quantise_x(0)
+            quantise(w1_grouped[:, halves], w1_codes[:, words], w1_scales[:, words])
+        w2_words = w2_sb[:].bitcast(F32).rearrange("n (q u) -> n u q", u=2)
+        w2_bank = psum_e.tile([P, 2, P], F32, name="w2_bank", tag="end0")
+        for u in range(2):
+            nc.tensor.transpose(w2_bank[:, u, :], w2_words[:, u, :], ident[:])
+        nc.scalar.copy(
+            out=w2_grouped[:].bitcast(F32).rearrange("q (n u) -> q n u", u=2),
+            in_=w2_bank[:].rearrange("q u n -> q n u"),
+        )
+        layer1(0)
+        transpose_x(1)
+        interleave_x(1)
+        quantise(w2_grouped[:], w2_codes[:], w2_scales[:])
+        nc.vector.reciprocal(out=inv_gain2[:], in_=gain2[:])
 
-        for step in range(-1, NCHUNK + 3):
+        for step in range(NCHUNK):
             run(transpose_x, step + 2)
             run(finish, step - 3)
             run(rotate, step - 2)
@@ -285,3 +324,17 @@ def tile_channel_net_pa_kernel(tc, x, noise, h, W1, b1, W2, b2, out):
             run(add_b2, step - 1)
             run(invert_norms, step - 2)
             run(regroup_a, step)
+
+        last = NCHUNK - 1
+        quantise_a(last)
+        layer2(last)
+        finish(last - 2)
+        rotate(last - 1)
+        add_b2(last)
+        sum_squares(last - 1)
+        invert_norms(last - 1)
+        rotate(last)
+        sum_squares(last)
+        finish(last - 1)
+        invert_norms(last)
+        finish(last)

@@ -39,11 +39,6 @@ def tile_channel_net_pa_kernel(tc, x, noise, h, W1, b1, W2, b2, out):
         h_bf = keep.tile([P, 2], BF16)
         b1_bf = keep.tile([P, PACK], BF16)
         b2_bf = keep.tile([P, 1], BF16)
-        with nc.allow_non_contiguous_dma(reason="three vectors of at most 1 KiB"):
-            nc.scalar.dma_start(out=b1_bf[:], in_=b1.rearrange("(q t) -> q t", t=PACK))
-            nc.scalar.dma_start(out=h_bf[:], in_=h.partition_broadcast(P))
-            nc.scalar.dma_start(out=b2_bf[:], in_=b2.rearrange("(q o) -> q o", o=1))
-
         x_cols = x.rearrange("(p r) k -> p (r k)", r=ROWS_PER_PARTITION)
         noise_rows = noise.rearrange("(p r) n -> p r n", r=ROWS_PER_PARTITION)
         out_rows = out.rearrange("(p r) n -> p r n", r=ROWS_PER_PARTITION)
@@ -64,7 +59,13 @@ def tile_channel_net_pa_kernel(tc, x, noise, h, W1, b1, W2, b2, out):
                     w1_t = keep.tile([P, D_IN], BF16, name="w1_%d" % t)
                     nc.sync.dma_start(out=w1_t[:], in_=w1_rows[:, t, :])
                     w1_sb.append(w1_t)
-                nc.sync.dma_start(out=w2_sb[:], in_=W2)
+                with nc.allow_non_contiguous_dma(reason="three vectors of at most 1 KiB"):
+                    nc.sync.dma_start(out=b1_bf[:], in_=b1.rearrange("(q t) -> q t", t=PACK))
+            if c == 1:
+                with nc.allow_non_contiguous_dma(reason="two vectors of at most 256 bytes"):
+                    nc.sync.dma_start(out=w2_sb[:], in_=W2)
+                    nc.sync.dma_start(out=h_bf[:], in_=h.partition_broadcast(P))
+                    nc.sync.dma_start(out=b2_bf[:], in_=b2.rearrange("(q o) -> q o", o=1))
             while len(noise_sb) * NOISE_TILES + NOISE_TILES // 2 < first + SIZES[c]:
                 n_first = len(noise_sb) * NOISE_TILES
                 n_g = keep.tile([P, NOISE_TILES, D_OUT], BF16, name="noise%d" % len(noise_sb))
@@ -82,8 +83,7 @@ def tile_channel_net_pa_kernel(tc, x, noise, h, W1, b1, W2, b2, out):
         nc.scalar.activation(out=one_root[:], in_=one[:], func=ACT.Abs_reciprocal_sqrt)
 
         b1_f = keep.tile([P, PACK], F32)
-        nc.vector.tensor_copy(out=b1_f[:], in_=b1_bf[:])
-
+        nc.gpsimd.tensor_copy(out=b1_f[:], in_=b1_bf[:])
         b2_f = keep.tile([P, 1], F32)
         nc.gpsimd.tensor_copy(out=b2_f[:], in_=b2_bf[:])
         h_f = keep.tile([P, 2], F32)
@@ -223,8 +223,12 @@ def tile_channel_net_pa_kernel(tc, x, noise, h, W1, b1, W2, b2, out):
                 a_scales[c][:, :n],
             )
 
+        def end_bank(c):
+            return (psum_t, "xt") if c == NCHUNK - 1 else (psum_e, "end%d" % (c % 2))
+
         def layer2(c):
-            zt_bank[c] = psum_e.tile([P, CHUNK], F32, name="zt_bank", tag="end%d" % (c % 2))
+            pool, tag = end_bank(c)
+            zt_bank[c] = pool.tile([P, CHUNK], F32, name="zt_bank", tag=tag)
             n = SIZES[c] * P
             nc.tensor.matmul_mx(
                 out=zt_bank[c][:, :n],
@@ -245,7 +249,8 @@ def tile_channel_net_pa_kernel(tc, x, noise, h, W1, b1, W2, b2, out):
             )
 
         def rotate(c):
-            y_bank[c] = psum_e.tile([P, TILES, D_OUT], F32, name="y_bank", tag="end%d" % (c % 2))
+            pool, tag = end_bank(c)
+            y_bank[c] = pool.tile([P, TILES, D_OUT], F32, name="y_bank", tag=tag)
             for i in range(SIZES[c]):
                 nc.tensor.matmul(
                     out=y_bank[c][:, i, :], lhsT=zt_sb[c][:, i * P : (i + 1) * P], rhs=tap[:],
@@ -281,10 +286,21 @@ def tile_channel_net_pa_kernel(tc, x, noise, h, W1, b1, W2, b2, out):
                 out=out_rows[:, FIRSTS[c] : FIRSTS[c] + SIZES[c], :], in_=result[:, : SIZES[c], :]
             )
 
+        idle = keep.tile([P, CHUNK], BF16)
+        nc.vector.memset(idle[:], 0.0)
+
+        def warm_up(times):
+            for turn in range(times):
+                bank = psum_e.tile([P, CHUNK], F32, name="warm_bank", tag="end1")
+                nc.tensor.matmul(
+                    out=bank[:], lhsT=idle[:, :P], rhs=idle[:], start=True, stop=True
+                )
+
         def run(stage, c):
             if 0 <= c < NCHUNK:
                 stage(c)
 
+        warm_up(5)
         transpose_x(0)
         interleave_x(0)
         for pair in range(PACK // 2):
@@ -296,6 +312,12 @@ def tile_channel_net_pa_kernel(tc, x, noise, h, W1, b1, W2, b2, out):
             if pair == 0:
                 quantise_x(0)
             quantise(w1_grouped[:, halves], w1_codes[:, words], w1_scales[:, words])
+        warm_up(2)
+        layer1(0)
+        relu(0)
+        transpose_x(1)
+        interleave_x(1)
+        quantise_x(1)
         w2_words = w2_sb[:].bitcast(F32).rearrange("n (q u) -> n u q", u=2)
         w2_bank = psum_e.tile([P, 2, P], F32, name="w2_bank", tag="end0")
         for u in range(2):
@@ -304,31 +326,26 @@ def tile_channel_net_pa_kernel(tc, x, noise, h, W1, b1, W2, b2, out):
             out=w2_grouped[:].bitcast(F32).rearrange("q (n u) -> q n u", u=2),
             in_=w2_bank[:].rearrange("q u n -> q n u"),
         )
-        layer1(0)
-        transpose_x(1)
-        interleave_x(1)
         quantise(w2_grouped[:], w2_codes[:], w2_scales[:])
         nc.vector.reciprocal(out=inv_gain2[:], in_=gain2[:])
 
         for step in range(NCHUNK):
             run(transpose_x, step + 2)
-            run(finish, step - 3)
             run(rotate, step - 2)
-            run(quantise_a, step - 1)
             run(layer2, step - 1)
-            run(quantise_x, step + 1)
-            run(relu, step)
             run(layer1, step + 1)
             run(interleave_x, step + 2)
+            run(regroup_a, step)
+            run(quantise_x, step + 2)
+            run(quantise_a, step)
             run(sum_squares, step - 2)
             run(add_b2, step - 1)
             run(invert_norms, step - 2)
-            run(regroup_a, step)
+            run(finish, step - 2)
+            run(relu, step + 1)
 
         last = NCHUNK - 1
-        quantise_a(last)
         layer2(last)
-        finish(last - 2)
         rotate(last - 1)
         add_b2(last)
         sum_squares(last - 1)

@@ -224,7 +224,7 @@ def tile_channel_net_pa_kernel(tc, x, noise, h, W1, b1, W2, b2, out):
             )
 
         def end_bank(c):
-            return (psum_t, "xt") if c == NCHUNK - 1 else (psum_e, "end%d" % (c % 2))
+            return (psum_t, "xt") if c >= NCHUNK - 2 else (psum_e, "end%d" % (c % 2))
 
         def layer2(c):
             pool, tag = end_bank(c)
@@ -274,7 +274,7 @@ def tile_channel_net_pa_kernel(tc, x, noise, h, W1, b1, W2, b2, out):
             )
 
         def finish(c):
-            result = work.tile([P, TILES, D_OUT], F32, name="result")
+            result = work.tile([P, TILES, D_OUT], F32, name="result", bufs=5)
             for i in range(SIZES[c]):
                 r = FIRSTS[c] + i
                 nc.vector.scalar_tensor_tensor(
@@ -300,7 +300,7 @@ def tile_channel_net_pa_kernel(tc, x, noise, h, W1, b1, W2, b2, out):
             if 0 <= c < NCHUNK:
                 stage(c)
 
-        warm_up(5)
+        warm_up(3)
         transpose_x(0)
         interleave_x(0)
         for pair in range(PACK // 2):
@@ -312,7 +312,7 @@ def tile_channel_net_pa_kernel(tc, x, noise, h, W1, b1, W2, b2, out):
             if pair == 0:
                 quantise_x(0)
             quantise(w1_grouped[:, halves], w1_codes[:, words], w1_scales[:, words])
-        warm_up(2)
+        warm_up(1)
         layer1(0)
         relu(0)
         transpose_x(1)
@@ -329,7 +329,7 @@ def tile_channel_net_pa_kernel(tc, x, noise, h, W1, b1, W2, b2, out):
         quantise(w2_grouped[:], w2_codes[:], w2_scales[:])
         nc.vector.reciprocal(out=inv_gain2[:], in_=gain2[:])
 
-        for step in range(NCHUNK):
+        for step in range(NCHUNK - 2):
             run(transpose_x, step + 2)
             run(rotate, step - 2)
             run(layer2, step - 1)
@@ -344,14 +344,32 @@ def tile_channel_net_pa_kernel(tc, x, noise, h, W1, b1, W2, b2, out):
             run(finish, step - 2)
             run(relu, step + 1)
 
-        last = NCHUNK - 1
-        layer2(last)
-        rotate(last - 1)
-        add_b2(last)
-        sum_squares(last - 1)
-        invert_norms(last - 1)
-        rotate(last)
-        sum_squares(last)
-        finish(last - 1)
-        invert_norms(last)
-        finish(last)
+        a, b = NCHUNK - 2, NCHUNK - 1
+        rotate(a - 2)
+        layer2(a - 1)
+        layer1(b)
+        add_b2(a - 1)
+        relu(b)
+        sum_squares(a - 2)
+        invert_norms(a - 2)
+        regroup_a(a)
+        quantise_a(a)
+        regroup_a(b)
+        quantise_a(b)
+        finish(a - 2)
+        rotate(a - 1)
+        layer2(a)
+        layer2(b)
+        add_b2(a)
+        sum_squares(a - 1)
+        invert_norms(a - 1)
+        add_b2(b)
+        finish(a - 1)
+        rotate(a)
+        rotate(b)
+        sum_squares(a)
+        invert_norms(a)
+        sum_squares(b)
+        invert_norms(b)
+        finish(a)
+        finish(b)

@@ -148,7 +148,8 @@ def tile_channel_net_pa_kernel(tc, x, noise, h, W1, b1, W2, b2, out):
         w2_scales = keep.tile([P, D_OUT], U8, align_bytes=64)
 
         x_banks, x_grouped, x_codes, x_scales = {}, {}, {}, {}
-        a_banks, a_planes, a_grouped, a_codes, a_scales = {}, {}, {}, {}, {}
+        plane_banks, tile_banks, a_planes, a_sums = {}, {}, {}, {}
+        a_grouped, a_codes, a_scales = {}, {}, {}
         zt_bank, zt_sb, y_bank, y_sums, y_scale = {}, {}, {}, {}, {}
 
         def transpose_x(c):
@@ -165,7 +166,7 @@ def tile_channel_net_pa_kernel(tc, x, noise, h, W1, b1, W2, b2, out):
         def interleave_x(c):
             x_grouped[c] = work.tile([P, CHUNK * PACK], BF16, name="x_grouped", align_bytes=64)
             for pair in range(SIZES[c] // 2):
-                on_scalar = pair == 1 and c % 2 == 0
+                on_scalar = c > 0
                 first = pair * PAIR * PACK
                 interleave_pair(
                     x_banks[c][pair],
@@ -179,38 +180,78 @@ def tile_channel_net_pa_kernel(tc, x, noise, h, W1, b1, W2, b2, out):
             n = SIZES[c] * P
             quantise(x_grouped[c][:, : n * PACK], x_codes[c][:, :n], x_scales[c][:, :n])
 
+        def split(c):
+            tiles = SIZES[c] // 2
+            return tiles * P, range(tiles, SIZES[c])
+
         def layer1(c):
-            a_banks[c] = []
-            n = SIZES[c] * P
-            for t in range(PACK):
-                bank = psum_a.tile([P, CHUNK], F32, name="a_bank", tag="a_bank")
+            n, tiles = split(c)
+
+            def multiply(dst, t, cols):
                 units = slice(t * P, (t + 1) * P)
                 nc.tensor.matmul_mx(
-                    out=bank[:, :n],
+                    out=dst,
                     lhsT=w1_codes[:, units].bitcast(FP8X4),
                     lhsT_scale=w1_scales[:, units],
-                    rhs=x_codes[c][:, :n].bitcast(FP8X4),
-                    rhs_scale=x_scales[c][:, :n],
+                    rhs=x_codes[c][:, cols].bitcast(FP8X4),
+                    rhs_scale=x_scales[c][:, cols],
                     start=True,
                     stop=True,
                 )
-                a_banks[c].append(bank)
+
+            plane_banks[c], tile_banks[c] = [], []
+            for pair in range(PACK // 2):
+                bank = psum_a.tile([P, 2, CHUNK // 2], F32, name="a_bank", tag="a_bank")
+                for e in range(2):
+                    multiply(bank[:, e, :n], 2 * pair + e, slice(0, n))
+                plane_banks[c].append(bank)
+            for i in tiles:
+                bank = psum_a.tile([P, PACK, P], F32, name="a_bank", tag="a_bank")
+                for t in range(PACK):
+                    multiply(bank[:, t, :], t, slice(i * P, (i + 1) * P))
+                tile_banks[c].append(bank)
 
         def relu(c):
-            a_planes[c] = work.tile([P, PACK, CHUNK], BF16, name="a_planes")
-            n = SIZES[c] * P
+            n, tiles = split(c)
+            a_planes[c] = work.tile([P, PACK, CHUNK // 2], BF16, name="a_planes")
             for t in range(PACK):
                 nc.scalar.activation(
-                    out=a_planes[c][:, t, :n], in_=a_banks[c][t][:, :n], func=ACT.Relu,
-                    bias=b1_f[:, t : t + 1], scale=1.0,
+                    out=a_planes[c][:, t, :n], in_=plane_banks[c][t // 2][:, t % 2, :n],
+                    func=ACT.Relu, bias=b1_f[:, t : t + 1], scale=1.0,
+                )
+
+        def add_b1(c):
+            n, tiles = split(c)
+            a_sums[c] = work.tile([P, CHUNK // 2, PACK], BF16, name="a_sums")
+            for k in range(len(tiles)):
+                nc.vector.tensor_tensor(
+                    out=a_sums[c][:, k * P : (k + 1) * P, :],
+                    in0=tile_banks[c][k][:].rearrange("q t b -> q b t"),
+                    in1=b1_f[:].unsqueeze(1).to_broadcast([P, P, PACK]),
+                    op=ALU.add,
                 )
 
         def regroup_a(c):
+            n, tiles = split(c)
             a_grouped[c] = work.tile([P, CHUNK, PACK], BF16, name="a_grouped", align_bytes=64)
-            n = SIZES[c] * P
+            m = n - P if SIZES[c] == TILES and c < NCHUNK - 2 else n
+            if m < n:
+                nc.gpsimd.tensor_scalar(
+                    out=a_grouped[c][:, m:n, :],
+                    in0=a_planes[c][:, :, m:n].rearrange("q t b -> q b t"),
+                    scalar1=1.0, scalar2=0.0, op0=ALU.mult, op1=ALU.add,
+                )
             nc.vector.tensor_copy(
-                out=a_grouped[c][:, :n, :].rearrange("q (c i) t -> q c t i", i=4),
-                in_=a_planes[c][:, :, :n].rearrange("q t (c i) -> q c t i", i=4),
+                out=a_grouped[c][:, :m, :].rearrange("q (c i) t -> q c t i", i=4),
+                in_=a_planes[c][:, :, :m].rearrange("q t (c i) -> q c t i", i=4),
+            )
+
+        def relu_sums(c):
+            n, tiles = split(c)
+            nc.vector.tensor_scalar(
+                out=a_grouped[c][:, n : SIZES[c] * P, :].rearrange("q b t -> q (b t)"),
+                in0=a_sums[c][:, : len(tiles) * P, :].rearrange("q b t -> q (b t)"),
+                scalar1=0.0, scalar2=None, op0=ALU.max,
             )
 
         def quantise_a(c):
@@ -315,6 +356,7 @@ def tile_channel_net_pa_kernel(tc, x, noise, h, W1, b1, W2, b2, out):
         warm_up(1)
         layer1(0)
         relu(0)
+        add_b1(0)
         transpose_x(1)
         interleave_x(1)
         quantise_x(1)
@@ -335,14 +377,16 @@ def tile_channel_net_pa_kernel(tc, x, noise, h, W1, b1, W2, b2, out):
             run(layer2, step - 1)
             run(layer1, step + 1)
             run(interleave_x, step + 2)
-            run(regroup_a, step)
+            run(regroup_a, step + 0)
+            run(relu_sums, step + 0)
             run(quantise_x, step + 2)
-            run(quantise_a, step)
+            run(quantise_a, step + 0)
             run(sum_squares, step - 2)
             run(add_b2, step - 1)
             run(invert_norms, step - 2)
             run(finish, step - 2)
             run(relu, step + 1)
+            run(add_b1, step + 1)
 
         a, b = NCHUNK - 2, NCHUNK - 1
         rotate(a - 2)
@@ -350,11 +394,14 @@ def tile_channel_net_pa_kernel(tc, x, noise, h, W1, b1, W2, b2, out):
         layer1(b)
         add_b2(a - 1)
         relu(b)
+        add_b1(b)
         sum_squares(a - 2)
         invert_norms(a - 2)
         regroup_a(a)
+        relu_sums(a)
         quantise_a(a)
         regroup_a(b)
+        relu_sums(b)
         quantise_a(b)
         finish(a - 2)
         rotate(a - 1)

@@ -21,6 +21,7 @@ SIZES = [TILES // 2] + [TILES] * (ROWS_PER_PARTITION // TILES - 1) + [TILES // 2
 FIRSTS = [sum(SIZES[:c]) for c in range(len(SIZES))]
 NCHUNK = len(SIZES)
 NOISE_TILES = 16
+LAG = 3
 TINY = 1e-30
 
 FLOPS = 2 * BATCH * D_IN * D_HID + 2 * BATCH * D_HID * D_OUT
@@ -166,7 +167,7 @@ def tile_channel_net_pa_kernel(tc, x, noise, h, W1, b1, W2, b2, out):
         def interleave_x(c):
             x_grouped[c] = work.tile([P, CHUNK * PACK], BF16, name="x_grouped", align_bytes=64)
             for pair in range(SIZES[c] // 2):
-                on_scalar = c > 0
+                on_scalar = c + pair > 1
                 first = pair * PAIR * PACK
                 interleave_pair(
                     x_banks[c][pair],
@@ -264,11 +265,8 @@ def tile_channel_net_pa_kernel(tc, x, noise, h, W1, b1, W2, b2, out):
                 a_scales[c][:, :n],
             )
 
-        def end_bank(c):
-            return (psum_t, "xt") if c >= NCHUNK - 2 else (psum_e, "end%d" % (c % 2))
-
         def layer2(c):
-            pool, tag = end_bank(c)
+            pool, tag = (psum_t, "xt") if c >= NCHUNK - 2 else (psum_e, "end%d" % (c % 2))
             zt_bank[c] = pool.tile([P, CHUNK], F32, name="zt_bank", tag=tag)
             n = SIZES[c] * P
             nc.tensor.matmul_mx(
@@ -282,7 +280,7 @@ def tile_channel_net_pa_kernel(tc, x, noise, h, W1, b1, W2, b2, out):
             )
 
         def add_b2(c):
-            zt_sb[c] = work.tile([P, CHUNK], F32, name="zt_sb")
+            zt_sb[c] = work.tile([P, CHUNK], F32, name="zt_sb", bufs=LAG + 2)
             n = SIZES[c] * P
             nc.scalar.activation(
                 out=zt_sb[c][:, :n], in_=zt_bank[c][:, :n], func=ACT.Identity, bias=b2_f[:],
@@ -290,7 +288,10 @@ def tile_channel_net_pa_kernel(tc, x, noise, h, W1, b1, W2, b2, out):
             )
 
         def rotate(c):
-            pool, tag = end_bank(c)
+            if c + LAG > NCHUNK - 2:
+                pool, tag = psum_a, "a_bank"
+            else:
+                pool, tag = psum_e, "end%d" % ((c + LAG) % 2)
             y_bank[c] = pool.tile([P, TILES, D_OUT], F32, name="y_bank", tag=tag)
             for i in range(SIZES[c]):
                 nc.tensor.matmul(
@@ -353,13 +354,12 @@ def tile_channel_net_pa_kernel(tc, x, noise, h, W1, b1, W2, b2, out):
             if pair == 0:
                 quantise_x(0)
             quantise(w1_grouped[:, halves], w1_codes[:, words], w1_scales[:, words])
-        warm_up(1)
-        layer1(0)
-        relu(0)
-        add_b1(0)
         transpose_x(1)
+        layer1(0)
         interleave_x(1)
+        relu(0)
         quantise_x(1)
+        add_b1(0)
         w2_words = w2_sb[:].bitcast(F32).rearrange("n (q u) -> n u q", u=2)
         w2_bank = psum_e.tile([P, 2, P], F32, name="w2_bank", tag="end0")
         for u in range(2):
@@ -373,50 +373,52 @@ def tile_channel_net_pa_kernel(tc, x, noise, h, W1, b1, W2, b2, out):
 
         for step in range(NCHUNK - 2):
             run(transpose_x, step + 2)
-            run(rotate, step - 2)
+            run(rotate, step - LAG)
             run(layer2, step - 1)
             run(layer1, step + 1)
             run(interleave_x, step + 2)
-            run(regroup_a, step + 0)
-            run(relu_sums, step + 0)
+            run(regroup_a, step)
+            run(relu_sums, step)
             run(quantise_x, step + 2)
-            run(quantise_a, step + 0)
-            run(sum_squares, step - 2)
+            run(quantise_a, step)
+            run(sum_squares, step - LAG)
             run(add_b2, step - 1)
-            run(invert_norms, step - 2)
-            run(finish, step - 2)
+            run(invert_norms, step - LAG)
+            run(finish, step - LAG)
             run(relu, step + 1)
             run(add_b1, step + 1)
 
         a, b = NCHUNK - 2, NCHUNK - 1
-        rotate(a - 2)
+        rotate(a - LAG)
         layer2(a - 1)
         layer1(b)
         add_b2(a - 1)
         relu(b)
-        add_b1(b)
-        sum_squares(a - 2)
-        invert_norms(a - 2)
+        sum_squares(a - LAG)
+        invert_norms(a - LAG)
         regroup_a(a)
         relu_sums(a)
+        add_b1(b)
         quantise_a(a)
         regroup_a(b)
         relu_sums(b)
         quantise_a(b)
+        finish(a - LAG)
+        rotate(a - 2)
+        layer2(a)
+        sum_squares(a - 2)
+        invert_norms(a - 2)
         finish(a - 2)
         rotate(a - 1)
-        layer2(a)
         layer2(b)
         add_b2(a)
         sum_squares(a - 1)
         invert_norms(a - 1)
-        add_b2(b)
         finish(a - 1)
+        add_b2(b)
         rotate(a)
         rotate(b)
-        sum_squares(a)
-        invert_norms(a)
-        sum_squares(b)
-        invert_norms(b)
-        finish(a)
-        finish(b)
+        for c in (a, b):
+            sum_squares(c)
+            invert_norms(c)
+            finish(c)

from contextlib import ExitStack

import concourse.masks as masks
import concourse.mybir as mybir

F32 = mybir.dt.float32
BF16 = mybir.dt.bfloat16
U32 = mybir.dt.uint32
U8 = mybir.dt.uint8
FP8X4 = mybir.dt.float8_e4m3fn_x4
ACT = mybir.ActivationFunctionType
ALU = mybir.AluOpType

P = 128
PACK = 4
BATCH, D_IN, D_HID, D_OUT = 8192, 512, 512, 128
CHUNK = 512
TILES = CHUNK // P
ROWS_PER_PARTITION = BATCH // P
SIZES = [TILES // 2] + [TILES] * (ROWS_PER_PARTITION // TILES - 1) + [TILES // 2]
FIRSTS = [sum(SIZES[:c]) for c in range(len(SIZES))]
NCHUNK = len(SIZES)
NOISE_TILES = 16
LAG = 3
TINY = 1e-30

FLOPS = 2 * BATCH * D_IN * D_HID + 2 * BATCH * D_HID * D_OUT


def tile_channel_net_pa_kernel(tc, x, noise, h, W1, b1, W2, b2, out):
    nc = tc.nc
    with ExitStack() as ctx:
        ctx.enter_context(tc.manual_schedule())
        keep = ctx.enter_context(tc.tile_pool(name="keep", bufs=1))
        work = ctx.enter_context(tc.tile_pool(name="work", bufs=3))
        psum_t = ctx.enter_context(tc.psum_pool(name="psum_t", bufs=2))
        psum_a = ctx.enter_context(tc.psum_pool(name="psum_a", bufs=PACK))
        psum_e = ctx.enter_context(tc.psum_pool(name="psum_e", bufs=1))

        h_bf = keep.tile([P, 2], BF16)
        b1_bf = keep.tile([P, PACK], BF16)
        b2_bf = keep.tile([P, 1], BF16)
        x_cols = x.rearrange("(p r) k -> p (r k)", r=ROWS_PER_PARTITION)
        noise_rows = noise.rearrange("(p r) n -> p r n", r=ROWS_PER_PARTITION)
        out_rows = out.rearrange("(p r) n -> p r n", r=ROWS_PER_PARTITION)
        w1_rows = W1.rearrange("(q t) k -> q t k", t=PACK)
        w1_sb = []
        w2_sb = keep.tile([P, D_HID], BF16)
        x_sb = []
        noise_sb = []
        for c in range(NCHUNK):
            first = FIRSTS[c]
            x_c = keep.tile([P, SIZES[c] * D_IN], BF16, name="x%d" % c)
            nc.sync.dma_start(
                out=x_c[:], in_=x_cols[:, first * D_IN : (first + SIZES[c]) * D_IN]
            )
            x_sb.append(x_c)
            if c == 0:
                for t in range(PACK):
                    w1_t = keep.tile([P, D_IN], BF16, name="w1_%d" % t)
                    nc.sync.dma_start(out=w1_t[:], in_=w1_rows[:, t, :])
                    w1_sb.append(w1_t)
                with nc.allow_non_contiguous_dma(reason="three vectors of at most 1 KiB"):
                    nc.sync.dma_start(out=b1_bf[:], in_=b1.rearrange("(q t) -> q t", t=PACK))
            if c == 1:
                with nc.allow_non_contiguous_dma(reason="two vectors of at most 256 bytes"):
                    nc.sync.dma_start(out=w2_sb[:], in_=W2)
                    nc.sync.dma_start(out=h_bf[:], in_=h.partition_broadcast(P))
                    nc.sync.dma_start(out=b2_bf[:], in_=b2.rearrange("(q o) -> q o", o=1))
            while len(noise_sb) * NOISE_TILES + NOISE_TILES // 2 < first + SIZES[c]:
                n_first = len(noise_sb) * NOISE_TILES
                n_g = keep.tile([P, NOISE_TILES, D_OUT], BF16, name="noise%d" % len(noise_sb))
                nc.sync.dma_start(
                    out=n_g[:], in_=noise_rows[:, n_first : n_first + NOISE_TILES, :]
                )
                noise_sb.append(n_g)

        ident = keep.tile([P, P], F32)
        masks.make_identity(nc, ident[:])

        one = keep.tile([P, 1], F32)
        nc.vector.memset(one[:], 1.0)
        one_root = keep.tile([P, 1], F32)
        nc.scalar.activation(out=one_root[:], in_=one[:], func=ACT.Abs_reciprocal_sqrt)

        b1_f = keep.tile([P, PACK], F32)
        nc.gpsimd.tensor_copy(out=b1_f[:], in_=b1_bf[:])
        b2_f = keep.tile([P, 1], F32)
        nc.gpsimd.tensor_copy(out=b2_f[:], in_=b2_bf[:])
        h_f = keep.tile([P, 2], F32)
        nc.gpsimd.tensor_copy(out=h_f[:], in_=h_bf[:])
        h_re = h_f[:, 0:1]
        h_im = h_f[:, 1:2]
        h_im_neg = keep.tile([P, 1], F32)
        nc.gpsimd.tensor_scalar(
            out=h_im_neg[:], in0=h_im, scalar1=-1.0, scalar2=None, op0=ALU.mult
        )

        h_sq = keep.tile([P, 2], F32)
        nc.gpsimd.tensor_tensor(out=h_sq[:], in0=h_f[:], in1=h_f[:], op=ALU.mult)
        h_abs2 = keep.tile([P, 1], F32)
        nc.gpsimd.tensor_tensor(out=h_abs2[:], in0=h_sq[:, 0:1], in1=h_sq[:, 1:2], op=ALU.add)
        gain2 = keep.tile([P, 1], F32)
        nc.gpsimd.tensor_scalar(
            out=gain2[:], in0=h_abs2[:], scalar1=float(D_OUT // 2), scalar2=TINY,
            op0=ALU.mult, op1=ALU.max,
        )
        inv_gain2 = keep.tile([P, 1], F32)

        tap_diag = keep.tile([P, P], F32)
        nc.gpsimd.tensor_scalar(
            out=tap_diag[:], in0=ident[:], scalar1=h_re, scalar2=0.0, op0=ALU.mult, op1=ALU.add,
        )
        tap_cross = keep.tile([P, P], F32)
        tap = keep.tile([P, P], F32)
        ident_pairs = ident[:].rearrange("n (j e) -> n j e", e=2)
        cross_pairs = tap_cross[:].rearrange("n (j e) -> n j e", e=2)
        nc.gpsimd.tensor_scalar(
            out=cross_pairs[:, :, 0], in0=ident_pairs[:, :, 1], scalar1=h_im_neg[:],
            scalar2=0.0, op0=ALU.mult, op1=ALU.add,
        )
        nc.gpsimd.tensor_scalar(
            out=cross_pairs[:, :, 1], in0=ident_pairs[:, :, 0], scalar1=h_im,
            scalar2=0.0, op0=ALU.mult, op1=ALU.add,
        )
        nc.gpsimd.tensor_tensor(out=tap[:], in0=tap_diag[:], in1=tap_cross[:], op=ALU.add)

        def transpose_pair(rows, bank):
            for i in range(2):
                words = rows[i].bitcast(F32).rearrange("b (q u) -> b u q", u=2)
                for u in range(2):
                    nc.tensor.transpose(bank[:, i, u, :], words[:, u, :], ident[:])

        def interleave_pair(bank, grouped, copy):
            copy(
                out=grouped.bitcast(F32).rearrange("q (i b u) -> q i b u", i=2, u=2),
                in_=bank[:].rearrange("q i u b -> q i b u"),
            )

        def quantise(grouped, codes, scales):
            nc.vector.quantize_mx(out=codes.bitcast(FP8X4), scales=scales, in_=grouped)

        PAIR = 2 * P
        w1_grouped = keep.tile([P, D_HID * PACK], BF16, align_bytes=64)
        w1_codes = keep.tile([P, D_HID], U32, align_bytes=64)
        w1_scales = keep.tile([P, D_HID], U8, align_bytes=64)
        w2_grouped = keep.tile([P, D_OUT * PACK], BF16, align_bytes=64)
        w2_codes = keep.tile([P, D_OUT], U32, align_bytes=64)
        w2_scales = keep.tile([P, D_OUT], U8, align_bytes=64)

        x_banks, x_grouped, x_codes, x_scales = {}, {}, {}, {}
        plane_banks, tile_banks, a_planes, a_sums = {}, {}, {}, {}
        a_grouped, a_codes, a_scales = {}, {}, {}
        zt_bank, zt_sb, y_bank, y_sums, y_scale = {}, {}, {}, {}, {}

        def transpose_x(c):
            x_banks[c] = []
            for pair in range(SIZES[c] // 2):
                bank = psum_t.tile([P, 2, 2, P], F32, name="xt", tag="xt")
                first = 2 * pair * D_IN
                transpose_pair(
                    [x_sb[c][:, first : first + D_IN], x_sb[c][:, first + D_IN : first + 2 * D_IN]],
                    bank,
                )
                x_banks[c].append(bank)

        def interleave_x(c):
            x_grouped[c] = work.tile([P, CHUNK * PACK], BF16, name="x_grouped", align_bytes=64)
            for pair in range(SIZES[c] // 2):
                on_scalar = c + pair > 1
                first = pair * PAIR * PACK
                interleave_pair(
                    x_banks[c][pair],
                    x_grouped[c][:, first : first + PAIR * PACK],
                    nc.scalar.copy if on_scalar else nc.vector.tensor_copy,
                )

        def quantise_x(c):
            x_codes[c] = work.tile([P, CHUNK], U32, name="x_codes", align_bytes=64)
            x_scales[c] = work.tile([P, CHUNK], U8, name="x_scales", align_bytes=64)
            n = SIZES[c] * P
            quantise(x_grouped[c][:, : n * PACK], x_codes[c][:, :n], x_scales[c][:, :n])

        def split(c):
            tiles = SIZES[c] // 2
            return tiles * P, range(tiles, SIZES[c])

        def layer1(c):
            n, tiles = split(c)

            def multiply(dst, t, cols):
                units = slice(t * P, (t + 1) * P)
                nc.tensor.matmul_mx(
                    out=dst,
                    lhsT=w1_codes[:, units].bitcast(FP8X4),
                    lhsT_scale=w1_scales[:, units],
                    rhs=x_codes[c][:, cols].bitcast(FP8X4),
                    rhs_scale=x_scales[c][:, cols],
                    start=True,
                    stop=True,
                )

            plane_banks[c], tile_banks[c] = [], []
            for pair in range(PACK // 2):
                bank = psum_a.tile([P, 2, CHUNK // 2], F32, name="a_bank", tag="a_bank")
                for e in range(2):
                    multiply(bank[:, e, :n], 2 * pair + e, slice(0, n))
                plane_banks[c].append(bank)
            for i in tiles:
                bank = psum_a.tile([P, PACK, P], F32, name="a_bank", tag="a_bank")
                for t in range(PACK):
                    multiply(bank[:, t, :], t, slice(i * P, (i + 1) * P))
                tile_banks[c].append(bank)

        def relu(c):
            n, tiles = split(c)
            a_planes[c] = work.tile([P, PACK, CHUNK // 2], BF16, name="a_planes")
            for t in range(PACK):
                nc.scalar.activation(
                    out=a_planes[c][:, t, :n], in_=plane_banks[c][t // 2][:, t % 2, :n],
                    func=ACT.Relu, bias=b1_f[:, t : t + 1], scale=1.0,
                )

        def add_b1(c):
            n, tiles = split(c)
            a_sums[c] = work.tile([P, CHUNK // 2, PACK], BF16, name="a_sums")
            for k in range(len(tiles)):
                nc.vector.tensor_tensor(
                    out=a_sums[c][:, k * P : (k + 1) * P, :],
                    in0=tile_banks[c][k][:].rearrange("q t b -> q b t"),
                    in1=b1_f[:].unsqueeze(1).to_broadcast([P, P, PACK]),
                    op=ALU.add,
                )

        def regroup_a(c):
            n, tiles = split(c)
            a_grouped[c] = work.tile([P, CHUNK, PACK], BF16, name="a_grouped", align_bytes=64)
            m = n - P if SIZES[c] == TILES and c < NCHUNK - 2 else n
            if m < n:
                nc.gpsimd.tensor_scalar(
                    out=a_grouped[c][:, m:n, :],
                    in0=a_planes[c][:, :, m:n].rearrange("q t b -> q b t"),
                    scalar1=1.0, scalar2=0.0, op0=ALU.mult, op1=ALU.add,
                )
            nc.vector.tensor_copy(
                out=a_grouped[c][:, :m, :].rearrange("q (c i) t -> q c t i", i=4),
                in_=a_planes[c][:, :, :m].rearrange("q t (c i) -> q c t i", i=4),
            )

        def relu_sums(c):
            n, tiles = split(c)
            nc.vector.tensor_scalar(
                out=a_grouped[c][:, n : SIZES[c] * P, :].rearrange("q b t -> q (b t)"),
                in0=a_sums[c][:, : len(tiles) * P, :].rearrange("q b t -> q (b t)"),
                scalar1=0.0, scalar2=None, op0=ALU.max,
            )

        def quantise_a(c):
            a_codes[c] = work.tile([P, CHUNK], U32, name="a_codes", align_bytes=64)
            a_scales[c] = work.tile([P, CHUNK], U8, name="a_scales", align_bytes=64)
            n = SIZES[c] * P
            quantise(
                a_grouped[c][:, :n, :].rearrange("q b t -> q (b t)"),
                a_codes[c][:, :n],
                a_scales[c][:, :n],
            )

        def layer2(c):
            pool, tag = (psum_t, "xt") if c >= NCHUNK - 2 else (psum_e, "end%d" % (c % 2))
            zt_bank[c] = pool.tile([P, CHUNK], F32, name="zt_bank", tag=tag)
            n = SIZES[c] * P
            nc.tensor.matmul_mx(
                out=zt_bank[c][:, :n],
                lhsT=w2_codes[:].bitcast(FP8X4),
                lhsT_scale=w2_scales[:],
                rhs=a_codes[c][:, :n].bitcast(FP8X4),
                rhs_scale=a_scales[c][:, :n],
                start=True,
                stop=True,
            )

        def add_b2(c):
            zt_sb[c] = work.tile([P, CHUNK], F32, name="zt_sb", bufs=LAG + 2)
            n = SIZES[c] * P
            nc.scalar.activation(
                out=zt_sb[c][:, :n], in_=zt_bank[c][:, :n], func=ACT.Identity, bias=b2_f[:],
                scale=1.0,
            )

        def rotate(c):
            if c + LAG > NCHUNK - 2:
                pool, tag = psum_a, "a_bank"
            else:
                pool, tag = psum_e, "end%d" % ((c + LAG) % 2)
            y_bank[c] = pool.tile([P, TILES, D_OUT], F32, name="y_bank", tag=tag)
            for i in range(SIZES[c]):
                nc.tensor.matmul(
                    out=y_bank[c][:, i, :], lhsT=zt_sb[c][:, i * P : (i + 1) * P], rhs=tap[:],
                    start=True, stop=True,
                )

        def sum_squares(c):
            squares = work.tile([P, TILES, D_OUT], BF16, name="squares")
            y_sums[c] = work.tile([P, TILES], F32, name="y_sums")
            for i in range(SIZES[c]):
                nc.scalar.activation(
                    out=squares[:, i, :], in_=y_bank[c][:, i, :], func=ACT.Square,
                    accum_out=y_sums[c][:, i : i + 1],
                )

        def invert_norms(c):
            y_scale[c] = work.tile([P, TILES], F32, name="y_scale")
            nc.scalar.activation(
                out=y_scale[c][:, : SIZES[c]], in_=y_sums[c][:, : SIZES[c]],
                func=ACT.Abs_reciprocal_sqrt, bias=TINY, scale=inv_gain2[:],
            )

        def finish(c):
            result = work.tile([P, TILES, D_OUT], F32, name="result", bufs=5)
            for i in range(SIZES[c]):
                r = FIRSTS[c] + i
                nc.vector.scalar_tensor_tensor(
                    out=result[:, i, :], in0=y_bank[c][:, i, :], scalar=y_scale[c][:, i : i + 1],
                    in1=noise_sb[r // NOISE_TILES][:, r % NOISE_TILES, :],
                    op0=ALU.mult, op1=ALU.add,
                )
            nc.sync.dma_start(
                out=out_rows[:, FIRSTS[c] : FIRSTS[c] + SIZES[c], :], in_=result[:, : SIZES[c], :]
            )

        idle = keep.tile([P, CHUNK], BF16)
        nc.vector.memset(idle[:], 0.0)

        def warm_up(times):
            for turn in range(times):
                bank = psum_e.tile([P, CHUNK], F32, name="warm_bank", tag="end1")
                nc.tensor.matmul(
                    out=bank[:], lhsT=idle[:, :P], rhs=idle[:], start=True, stop=True
                )

        def run(stage, c):
            if 0 <= c < NCHUNK:
                stage(c)

        warm_up(3)
        transpose_x(0)
        interleave_x(0)
        for pair in range(PACK // 2):
            w1_bank = psum_a.tile([P, 2, 2, P], F32, name="w1_bank", tag="a_bank")
            transpose_pair([w1_sb[2 * pair][:], w1_sb[2 * pair + 1][:]], w1_bank)
            words = slice(pair * PAIR, (pair + 1) * PAIR)
            halves = slice(pair * PAIR * PACK, (pair + 1) * PAIR * PACK)
            interleave_pair(w1_bank, w1_grouped[:, halves], nc.scalar.copy)
            if pair == 0:
                quantise_x(0)
            quantise(w1_grouped[:, halves], w1_codes[:, words], w1_scales[:, words])
        transpose_x(1)
        layer1(0)
        interleave_x(1)
        relu(0)
        quantise_x(1)
        add_b1(0)
        w2_words = w2_sb[:].bitcast(F32).rearrange("n (q u) -> n u q", u=2)
        w2_bank = psum_e.tile([P, 2, P], F32, name="w2_bank", tag="end0")
        for u in range(2):
            nc.tensor.transpose(w2_bank[:, u, :], w2_words[:, u, :], ident[:])
        nc.scalar.copy(
            out=w2_grouped[:].bitcast(F32).rearrange("q (n u) -> q n u", u=2),
            in_=w2_bank[:].rearrange("q u n -> q n u"),
        )
        quantise(w2_grouped[:], w2_codes[:], w2_scales[:])
        nc.vector.reciprocal(out=inv_gain2[:], in_=gain2[:])

        for step in range(NCHUNK - 2):
            run(transpose_x, step + 2)
            run(rotate, step - LAG)
            run(layer2, step - 1)
            run(layer1, step + 1)
            run(interleave_x, step + 2)
            run(regroup_a, step)
            run(relu_sums, step)
            run(quantise_x, step + 2)
            run(quantise_a, step)
            run(sum_squares, step - LAG)
            run(add_b2, step - 1)
            run(invert_norms, step - LAG)
            run(finish, step - LAG)
            run(relu, step + 1)
            run(add_b1, step + 1)

        a, b = NCHUNK - 2, NCHUNK - 1
        rotate(a - LAG)
        layer2(a - 1)
        layer1(b)
        add_b2(a - 1)
        relu(b)
        sum_squares(a - LAG)
        invert_norms(a - LAG)
        regroup_a(a)
        relu_sums(a)
        add_b1(b)
        quantise_a(a)
        regroup_a(b)
        relu_sums(b)
        quantise_a(b)
        finish(a - LAG)
        rotate(a - 2)
        layer2(a)
        sum_squares(a - 2)
        invert_norms(a - 2)
        finish(a - 2)
        rotate(a - 1)
        layer2(b)
        add_b2(a)
        sum_squares(a - 1)
        invert_norms(a - 1)
        finish(a - 1)
        add_b2(b)
        rotate(a)
        rotate(b)
        for c in (a, b):
            sum_squares(c)
            invert_norms(c)
            finish(c)
